import numpy as np
import ml_dtypes


def mxq(x, axis, fmt="e4m3"):
    dtype, down = {"e4m3": (ml_dtypes.float8_e4m3fn, 7), "e5m2": (ml_dtypes.float8_e5m2, 14)}[fmt]
    v = np.moveaxis(np.asarray(x, np.float32).astype(ml_dtypes.bfloat16).astype(np.float64), axis, -1)
    blocks = v.reshape(v.shape[:-1] + (-1, 32))
    amax = np.abs(blocks).max(-1, keepdims=True)
    byte = np.maximum(np.where(amax > 0, np.frexp(amax)[1] - 1 + 127, 0) - down, 1)
    scale = np.exp2(byte - 127.0)
    codes = (blocks / scale).astype(np.float32).astype(dtype).astype(np.float64)
    return np.moveaxis((codes * scale).reshape(v.shape), -1, axis)


WIDE = False


def mx_kscale(k):
    if not WIDE:
        return np.ones(k)
    levels = np.array([10, -10, 5, -5, 0])
    a = np.random.permutation(np.resize(levels, k // 512 * 4)).reshape(k // 512, 4)
    idx = np.arange(k)
    return np.exp2(a[idx // 512, idx % 128 // 32])


BF16 = ml_dtypes.bfloat16


def bf(x):
    return np.asarray(x, np.float32).astype(BF16)


def f64(x):
    return np.asarray(x).astype(np.float64)


B, T, U, H = 4, 64, 32, 512
INNER, VOCAB = 512, 1024


def log_softmax(v):
    sh = v - v.max(-1, keepdims=True)
    return sh - np.log(np.exp(sh).sum(-1, keepdims=True))


def setup_inputs():
    s = mx_kscale(2 * H)
    return {"enc_state": bf(np.random.standard_normal((B, T, H)) * s[:H]),
            "dec_state": bf(np.random.standard_normal((B, U, H)) * s[H:]),
            "W1": bf(np.random.standard_normal((2 * H, INNER)) / np.sqrt(2.0 * H) / s[:, None]),
            "b1": bf(np.random.standard_normal(INNER) * 0.2),
            "W2": bf(np.random.standard_normal((INNER, VOCAB)) * 0.06),
            "b2": bf(np.random.standard_normal(VOCAB) * 0.2)}


def reference(enc_state, dec_state, W1, b1, W2, b2):
    W1 = f64(W1)
    enc_proj = mxq(f64(enc_state), 2, "e4m3") @ mxq(W1[:H], 0, "e4m3")
    dec_proj = mxq(f64(dec_state), 2, "e4m3") @ mxq(W1[H:], 0, "e4m3")
    hidden = np.tanh(enc_proj[:, :, None, :] + dec_proj[:, None, :, :] + f64(b1))
    logits = (mxq(hidden, 3, "e4m3") @ mxq(f64(W2), 0, "e4m3")) + f64(b2)
    return log_softmax(logits)

@@ -1,0 +1,382 @@
+from contextlib import ExitStack
+
+import concourse.masks as masks
+import concourse.mybir as mybir
+
+F32 = mybir.dt.float32
+BF16 = mybir.dt.bfloat16
+U32 = mybir.dt.uint32
+U8 = mybir.dt.uint8
+I32 = mybir.dt.int32
+FP8X4 = mybir.dt.float8_e4m3fn_x4
+ALU = mybir.AluOpType
+ACT = mybir.ActivationFunctionType
+AX = mybir.AxisListType
+
+P = 128
+FLOPS = 2 * (256 * 512 * 512 + 128 * 512 * 512 + 8192 * 512 * 1024)
+LN2 = 0.6931471805599453
+
+
+def make_plan(groups, modes, batches, look, prep_lead):
+    look_add, look_tanh, look_quant, look_mx, lag_red, lag_exp = look
+    n_groups = len(groups)
+    n_tiles = sum(n for (f, n) in groups)
+    group_of = {}
+    for g, (f, n) in enumerate(groups):
+        for t in range(f, f + n):
+            group_of[t] = g
+    last_b = {}
+    for b, (f, n) in enumerate(batches):
+        last_b[f + n - 1] = b
+    prep_at = {}
+    prepared = set()
+    for g, (f, n) in enumerate(groups):
+        if modes[g] != "P" and (f // 16) not in prepared:
+            prepared.add(f // 16)
+            prep_at[max(f - prep_lead, 0)] = f // 16
+    plan = []
+    st = {"add": 0, "tanh": 0, "quant": 0, "mx": 0}
+    for k in range(-look_add, n_tiles + lag_exp + 1):
+        while st["add"] < n_tiles and st["add"] <= k + look_add:
+            t = st["add"]
+            g = group_of[t]
+            if t in prep_at:
+                plan.append(("prep", prep_at[t]))
+            if modes[g] == "P":
+                plan.append(("padd", t))
+            elif t == groups[g][0]:
+                plan.append(("add", g))
+            st["add"] += 1
+        while st["tanh"] < st["add"] and st["tanh"] <= k + look_tanh:
+            t = st["tanh"]
+            g = group_of[t]
+            if modes[g] == "P":
+                plan.append(("ptanh", t))
+            elif t == groups[g][0]:
+                plan.append(("tanh", g))
+            st["tanh"] += 1
+        while st["quant"] < n_groups:
+            f, n = groups[st["quant"]]
+            if f + n - 1 < st["tanh"] and f + n - 1 <= k + look_quant:
+                plan.append(("quant", st["quant"]))
+                st["quant"] += 1
+            else:
+                break
+        while st["mx"] < n_tiles and st["mx"] <= k + look_mx and group_of[st["mx"]] < st["quant"]:
+            plan.append(("mx", st["mx"]))
+            st["mx"] += 1
+        if 0 <= k < n_tiles:
+            assert st["mx"] > k, (k, st)
+            plan.append(("ev", k, 0))
+            plan.append(("ev", k, 1))
+        if 0 <= k - lag_red < n_tiles:
+            plan.append(("red", k - lag_red))
+        t = k - lag_exp
+        if 0 <= t < n_tiles:
+            plan.append(("exp", t))
+            if t in last_b:
+                b = last_b[t]
+                plan.append(("ln", b))
+                f, n = batches[b]
+                for u in range(f, f + n):
+                    plan.append(("fin", u))
+    return plan
+
+
+def spans(sizes):
+    out = []
+    f = 0
+    for n in sizes:
+        out.append((f, n))
+        f += n
+    return out
+
+
+GROUPS = spans([1, 1] + [2] * 31)
+VECTOR_TILES = (22, 24, 38, 40, 52, 54)
+MODES = [("G" if f in VECTOR_TILES else "P") for (f, n) in GROUPS]
+BATCHES = spans([8] * 7 + [4, 4])
+LOOK = (8, 6, 4, 3, 1, 2)
+FIN_VECTOR_FROM = 60
+
+
+def tile_transducer_kernel(tc, enc_state, dec_state, W1, b1, W2, b2, out):
+    nc = tc.nc
+    enc2 = enc_state.flatten_outer_dims()
+    dec2 = dec_state.flatten_outer_dims()
+    outf = out.flatten_outer_dims()
+    plan = make_plan(GROUPS, MODES, BATCHES, LOOK, 8)
+    group_of = {}
+    for g, (f, n) in enumerate(GROUPS):
+        for t in range(f, f + n):
+            group_of[t] = g
+    batch_of = {}
+    for b, (f, n) in enumerate(BATCHES):
+        for t in range(f, f + n):
+            batch_of[t] = b
+
+    with ExitStack() as ctx:
+        const = ctx.enter_context(tc.tile_pool(name="const", bufs=1))
+        work = ctx.enter_context(tc.tile_pool(name="work", bufs=3))
+        zpool = ctx.enter_context(tc.tile_pool(name="zpool", bufs=24))
+        small = ctx.enter_context(tc.tile_pool(name="small", bufs=9))
+        ps = ctx.enter_context(tc.psum_pool(name="ps", bufs=6))
+        ctx.enter_context(tc.manual_schedule())
+
+        enc_sb = const.tile([P, 2, 512], BF16, name="enc_sb")
+        nc.sync.dma_start(out=enc_sb[:], in_=enc2.rearrange("(s p) h -> p s h", p=P))
+        dec_sb = const.tile([P, 512], BF16, name="dec_sb")
+        nc.sync.dma_start(out=dec_sb[:], in_=dec2)
+        b1_st = const.tile([P, 512], BF16, name="b1_st")
+        nc.sync.dma_start(out=b1_st[96:97, :], in_=b1.rearrange("(o c) -> o c", o=1))
+        raw1 = const.tile([P, 2, 4, 512], BF16, name="raw1")
+        for a in range(2):
+            nc.sync.dma_start(
+                out=raw1[:, a].rearrange("p (u e) c -> p u e c", u=2),
+                in_=W1[a * 512 : (a + 1) * 512, :].rearrange("(u q e) c -> q u e c", u=2, e=2),
+            )
+        raw2 = const.tile([P, 4, 1024], BF16, name="raw2")
+        nc.sync.dma_start(out=raw2[:], in_=W2.rearrange("(p j) v -> p j v", j=4))
+        b2_bc = const.tile([P, 1024], BF16, name="b2_bc")
+        nc.sync.dma_start(out=b2_bc[:], in_=b2.partition_broadcast(P))
+
+        ident = const.tile([P, P], F32, name="ident")
+        masks.make_identity(nc, ident[:])
+        xg = const.tile([P, 4096], BF16, name="xg", align_bytes=64)
+        nc.gpsimd.memset(xg[:].bitcast(F32), 0.0)
+        b1row = const.tile([P, 512], F32, name="b1row")
+        nc.gpsimd.memset(b1row[:], 0.0)
+
+        warm = const.tile([P, 1], F32, name="warm")
+        nc.vector.memset(warm[:], 0.0)
+        warm2 = const.tile([P, 1], F32, name="warm2")
+        nc.scalar.activation(out=warm2[:], in_=warm[:], func=ACT.Exp)
+
+        sel = const.tile([P, 2048], F32, name="sel")
+        nc.vector.scalar_tensor_tensor(
+            out=sel[:].rearrange("p (c u) -> p c u", u=32),
+            in0=ident[:, 0:64].unsqueeze(2).to_broadcast([P, 64, 32]),
+            scalar=ident[:, 96:97],
+            in1=ident[:, 64:96].unsqueeze(1).to_broadcast([P, 64, 32]),
+            op0=ALU.add,
+            op1=ALU.add,
+        )
+        nc.vector.tensor_copy(
+            out=b1row[96:97, :].rearrange("o (j m) -> o j m", j=4),
+            in_=b1_st[96:97, :].rearrange("o (m j) -> o j m", j=4),
+        )
+
+        xt_e = ps.tile([P, 512], F32, tag="lg", name="xt_e")
+        for s in range(2):
+            for u in range(2):
+                nc.tensor.transpose(
+                    out=xt_e[:, (2 * s + u) * P : (2 * s + u + 1) * P],
+                    in_=enc_sb[:, s, :].bitcast(F32)[:, u * P : (u + 1) * P],
+                    identity=ident[:],
+                )
+        xt_d = ps.tile([P, 512], F32, tag="lg", name="xt_d")
+        for u in range(2):
+            nc.tensor.transpose(
+                out=xt_d[:, u * P : (u + 1) * P],
+                in_=dec_sb[:].bitcast(F32)[:, u * P : (u + 1) * P],
+                identity=ident[:],
+            )
+        xgf = xg[:].bitcast(F32).rearrange("p (a c u) -> p a c u", a=8, u=2)
+        for s in range(2):
+            nc.vector.tensor_copy(
+                out=xgf[:, 2 * s : 2 * s + 2, 0:64, :],
+                in_=xt_e[:, s * 256 : (s + 1) * 256].rearrange("p (u b t) -> p b t u", u=2, b=2),
+            )
+        nc.vector.tensor_copy(
+            out=xgf[:, 4:8, 64:96, :],
+            in_=xt_d[:, 0:256].rearrange("p (e b u) -> p b u e", e=2, b=4),
+        )
+        xc = const.tile([P, 1024], U32, name="xc", align_bytes=64)
+        xs = const.tile([P, 1024], U8, name="xs", align_bytes=64)
+        for a in range(2):
+            nc.vector.quantize_mx(
+                out=xc[:, a * 512 : (a + 1) * 512].bitcast(FP8X4),
+                scales=xs[:, a * 512 : (a + 1) * 512],
+                in_=xg[:, a * 2048 : (a + 1) * 2048],
+            )
+
+        g1 = const.tile([P, 2, 2048], BF16, name="g1", align_bytes=64)
+        w1c = const.tile([P, 1024], U32, name="w1c", align_bytes=64)
+        w1s = const.tile([P, 1024], U8, name="w1s", align_bytes=64)
+        nc.vector.tensor_copy(
+            out=g1[:, 0, :].rearrange("p (j m t) -> p j m t", j=4, t=4),
+            in_=raw1[:, 0].rearrange("p t (m j) -> p j m t", j=4),
+        )
+        nc.scalar.copy(
+            out=g1[:, 1, :].rearrange("p (j m t) -> p j m t", j=4, t=4),
+            in_=raw1[:, 1].rearrange("p t (m j) -> p j m t", j=4),
+        )
+        for a in range(2):
+            nc.vector.quantize_mx(
+                out=w1c[:, a * 512 : (a + 1) * 512].bitcast(FP8X4),
+                scales=w1s[:, a * 512 : (a + 1) * 512],
+                in_=g1[:, a, :],
+            )
+
+        pmat = const.tile([P, 4, 512], F32, name="pmat")
+        pp = []
+        for b in range(4):
+            acc = ps.tile([P, 512], F32, tag="lg", name="pp%d" % b)
+            pp.append(acc)
+            for a in range(2):
+                o = (4 * a + b) * P
+                nc.tensor.matmul_mx(
+                    out=acc[:],
+                    lhsT=xc[:, o : o + P].bitcast(FP8X4),
+                    lhsT_scale=xs[:, o : o + P],
+                    rhs=w1c[:, a * 512 : (a + 1) * 512].bitcast(FP8X4),
+                    rhs_scale=w1s[:, a * 512 : (a + 1) * 512],
+                    start=(a == 0),
+                    stop=(a == 1),
+                )
+        nc.vector.tensor_tensor(out=pmat[:, 0, :], in0=pp[0][:], in1=b1row[:], op=ALU.add)
+
+        g2 = const.tile([P, 4096], BF16, name="g2", align_bytes=64)
+        w2c = const.tile([P, 1024], U32, name="w2c", align_bytes=64)
+        w2s = const.tile([P, 1024], U8, name="w2s", align_bytes=64)
+        nc.vector.tensor_copy(
+            out=g2[:, 0:2048].rearrange("p (v j) -> p v j", j=4),
+            in_=raw2[:, :, 0:512].rearrange("p j v -> p v j"),
+        )
+        nc.scalar.copy(
+            out=g2[:, 2048:4096].rearrange("p (v j) -> p v j", j=4),
+            in_=raw2[:, :, 512:1024].rearrange("p j v -> p v j"),
+        )
+        nc.vector.quantize_mx(out=w2c[:].bitcast(FP8X4), scales=w2s[:], in_=g2[:])
+        b2f = const.tile([P, 1024], F32, name="b2f")
+        nc.gpsimd.tensor_scalar(out=b2f[:], in0=b2_bc[:], scalar1=1.0, scalar2=0.0, op0=ALU.mult, op1=ALU.add)
+        for b in range(1, 4):
+            nc.vector.tensor_tensor(out=pmat[:, b, :], in0=pp[b][:], in1=b1row[:], op=ALU.add)
+
+        ed = {}
+        pbank = {}
+        pre = {}
+        hid = {}
+        hcod = {}
+        hsc = {}
+        lg = {}
+        zt = {}
+        bt = {}
+
+        def batch_tiles(b):
+            if b not in bt:
+                d = {}
+                for nm in ("negm", "ssum", "lns", "negc"):
+                    d[nm] = small.tile([P, 8], F32, tag=nm, name="%s%d" % (nm, b))
+                bt[b] = d
+            return bt[b]
+
+        def hid_tile(g):
+            if g not in hid:
+                hid[g] = work.tile([P, 2 * 512], BF16, tag="hid", name="hid%d" % g, align_bytes=64)
+            return hid[g]
+
+        for op in plan:
+            kind = op[0]
+            if kind == "prep":
+                b = op[1]
+                tr = ps.tile([P, 512], F32, tag="lg", name="tr%d" % b)
+                for j in range(4):
+                    nc.tensor.transpose(out=tr[:, j * P : (j + 1) * P], in_=pmat[:, b, j * P : (j + 1) * P], identity=ident[:])
+                e = const.tile([P, P, 4], F32, name="ed%d" % b)
+                ed[b] = e
+                nc.scalar.copy(out=e[:], in_=tr[:].rearrange("p (j n) -> p n j", j=4))
+                nc.gpsimd.tensor_tensor(out=e[:, 0:64, :], in0=e[:, 0:64, :], in1=e[:, 96:97, :].to_broadcast([P, 64, 4]), op=ALU.add)
+            elif kind == "padd":
+                t = op[1]
+                b = t // 16
+                c0 = (t % 16) * P
+                pb = ps.tile([P, 512], F32, tag="pb", bufs=2, name="pb%d" % t)
+                pbank[t] = pb
+                for j in range(4):
+                    nc.tensor.matmul(out=pb[:, j * P : (j + 1) * P], lhsT=pmat[:, b, j * P : (j + 1) * P], rhs=sel[:, c0 : c0 + P], start=True, stop=True)
+            elif kind == "ptanh":
+                t = op[1]
+                g = group_of[t]
+                s = t - GROUPS[g][0]
+                h = hid_tile(g)
+                nc.scalar.activation(
+                    out=h[:, s * 512 : (s + 1) * 512].rearrange("p (r j) -> p r j", j=4),
+                    in_=pbank[t][:].rearrange("p (j r) -> p r j", j=4),
+                    func=ACT.Tanh,
+                )
+            elif kind == "add":
+                g = op[1]
+                f, n = GROUPS[g]
+                b = f // 16
+                t0 = (f % 16) * 4
+                nt = 4 * n
+                pr = work.tile([P, 2 * 512], F32, tag="pre", bufs=2, name="pre%d" % g)
+                pre[g] = pr
+                eng = nc.vector if MODES[g] == "V" else nc.gpsimd
+                eng.tensor_tensor(
+                    out=pr[:, : nt * P].rearrange("p (t u j) -> p t u j", u=32, j=4),
+                    in0=ed[b][:, 64:96, :].unsqueeze(1).to_broadcast([P, nt, 32, 4]),
+                    in1=ed[b][:, t0 : t0 + nt, :].unsqueeze(2).to_broadcast([P, nt, 32, 4]),
+                    op=ALU.add,
+                )
+            elif kind == "tanh":
+                g = op[1]
+                n = GROUPS[g][1]
+                nc.scalar.activation(out=hid_tile(g)[:, : n * 512], in_=pre[g][:, : n * 512], func=ACT.Tanh)
+            elif kind == "quant":
+                g = op[1]
+                n = GROUPS[g][1]
+                hcod[g] = work.tile([P, 2 * P], U32, tag="hc", name="hc%d" % g, align_bytes=64)
+                hsc[g] = work.tile([P, 2 * P], U8, tag="hs", name="hs%d" % g, align_bytes=64)
+                nc.vector.quantize_mx(out=hcod[g][:, : n * P].bitcast(FP8X4), scales=hsc[g][:, : n * P], in_=hid[g][:, : n * 512])
+            elif kind == "mx":
+                t = op[1]
+                g = group_of[t]
+                s = t - GROUPS[g][0]
+                for h in range(2):
+                    acc = ps.tile([P, 512], F32, tag="lg", name="lg%d_%d" % (t, h))
+                    lg[(t, h)] = acc
+                    nc.tensor.matmul_mx(
+                        out=acc[:],
+                        lhsT=hcod[g][:, s * P : (s + 1) * P].bitcast(FP8X4),
+                        lhsT_scale=hsc[g][:, s * P : (s + 1) * P],
+                        rhs=w2c[:, h * 512 : (h + 1) * 512].bitcast(FP8X4),
+                        rhs_scale=w2s[:, h * 512 : (h + 1) * 512],
+                        start=True,
+                        stop=True,
+                    )
+            elif kind == "ev":
+                t, h = op[1], op[2]
+                if h == 0:
+                    zt[t] = zpool.tile([P, 1024], F32, tag="z", name="z%d" % t)
+                nc.vector.tensor_tensor(out=zt[t][:, h * 512 : (h + 1) * 512], in0=lg[(t, h)][:], in1=b2f[:, h * 512 : (h + 1) * 512], op=ALU.add)
+            elif kind == "red":
+                t = op[1]
+                b = batch_of[t]
+                c = t - BATCHES[b][0]
+                nc.vector.tensor_reduce(out=batch_tiles(b)["negm"][:, c : c + 1], in_=zt[t][:], axis=AX.X, op=ALU.max, negate=True)
+            elif kind == "exp":
+                t = op[1]
+                b = batch_of[t]
+                c = t - BATCHES[b][0]
+                d = batch_tiles(b)
+                junk = work.tile([P, 1024], BF16, tag="junk", bufs=2, name="junk%d" % t)
+                nc.scalar.activation(out=junk[:], in_=zt[t][:], func=ACT.Exp, bias=d["negm"][:, c : c + 1], scale=1.0, accum_out=d["ssum"][:, c : c + 1])
+            elif kind == "ln":
+                b = op[1]
+                n = BATCHES[b][1]
+                d = batch_tiles(b)
+                nc.scalar.activation(out=d["lns"][:, :n], in_=d["ssum"][:, :n], func=ACT.Ln)
+                nc.gpsimd.tensor_tensor(out=d["negc"][:, :n], in0=d["negm"][:, :n], in1=d["lns"][:, :n], op=ALU.subtract)
+            else:
+                t = op[1]
+                b = batch_of[t]
+                c = t - BATCHES[b][0]
+                negc = batch_tiles(b)["negc"][:, c : c + 1]
+                if t >= FIN_VECTOR_FROM:
+                    nc.vector.tensor_scalar(out=zt[t][:], in0=zt[t][:], scalar1=negc, scalar2=None, op0=ALU.add)
+                else:
+                    nc.gpsimd.tensor_scalar(out=zt[t][:], in0=zt[t][:], scalar1=1.0, scalar2=negc, op0=ALU.mult, op1=ALU.add)
+                nc.sync.dma_start(out=outf[t * P : (t + 1) * P, :], in_=zt[t][:])

@@ -15,11 +15,10 @@ AX = mybir.AxisListType
 
 P = 128
 FLOPS = 2 * (256 * 512 * 512 + 128 * 512 * 512 + 8192 * 512 * 1024)
-LN2 = 0.6931471805599453
 
 
-def make_plan(groups, modes, batches, look, prep_lead):
-    look_add, look_tanh, look_quant, look_mx, lag_red, lag_exp = look
+def make_plan(groups, modes, batches, look, start, prep_lead, fins_a_step):
+    look_add, look_tanh, look_quant, look_mx, lag_exp = look
     n_groups = len(groups)
     n_tiles = sum(n for (f, n) in groups)
     group_of = {}
@@ -36,9 +35,18 @@ def make_plan(groups, modes, batches, look, prep_lead):
             prepared.add(f // 16)
             prep_at[max(f - prep_lead, 0)] = f // 16
     plan = []
-    st = {"add": 0, "tanh": 0, "quant": 0, "mx": 0}
-    for k in range(-look_add, n_tiles + lag_exp + 1):
-        while st["add"] < n_tiles and st["add"] <= k + look_add:
+    for t in range(start):
+        plan.append(("padd", t))
+        plan.append(("ptanh", t))
+        if t >= 1:
+            plan.append(("quant", t - 1))
+            plan.append(("mx", t - 1))
+    st = {"add": start, "tanh": start, "quant": start - 1, "mx": start - 1, "exp": 0, "fin": 0}
+    fins = []
+    k = 0
+    while st["fin"] < n_tiles:
+        less = max(0, look_add - start - (k + 1) // 2)
+        while st["add"] < n_tiles and st["add"] <= k + look_add - less:
             t = st["add"]
             g = group_of[t]
             if t in prep_at:
@@ -48,7 +56,7 @@ def make_plan(groups, modes, batches, look, prep_lead):
             elif t == groups[g][0]:
                 plan.append(("add", g))
             st["add"] += 1
-        while st["tanh"] < st["add"] and st["tanh"] <= k + look_tanh:
+        while st["tanh"] < st["add"] and st["tanh"] <= k + look_tanh - less:
             t = st["tanh"]
             g = group_of[t]
             if modes[g] == "P":
@@ -58,7 +66,7 @@ def make_plan(groups, modes, batches, look, prep_lead):
             st["tanh"] += 1
         while st["quant"] < n_groups:
             f, n = groups[st["quant"]]
-            if f + n - 1 < st["tanh"] and f + n - 1 <= k + look_quant:
+            if f + n - 1 < st["tanh"] and f + n - 1 <= k + max(look_quant - less, 1):
                 plan.append(("quant", st["quant"]))
                 st["quant"] += 1
             else:
@@ -66,21 +74,26 @@ def make_plan(groups, modes, batches, look, prep_lead):
         while st["mx"] < n_tiles and st["mx"] <= k + look_mx and group_of[st["mx"]] < st["quant"]:
             plan.append(("mx", st["mx"]))
             st["mx"] += 1
-        if 0 <= k < n_tiles:
+        if k < n_tiles:
             assert st["mx"] > k, (k, st)
             plan.append(("ev", k, 0))
             plan.append(("ev", k, 1))
-        if 0 <= k - lag_red < n_tiles:
-            plan.append(("red", k - lag_red))
-        t = k - lag_exp
-        if 0 <= t < n_tiles:
+        if 0 <= k - 1 < n_tiles:
+            plan.append(("red", k - 1))
+        while st["exp"] < min(k, n_tiles) and (st["exp"] <= k - lag_exp or k >= n_tiles):
+            t = st["exp"]
             plan.append(("exp", t))
+            st["exp"] += 1
             if t in last_b:
                 b = last_b[t]
                 plan.append(("ln", b))
                 f, n = batches[b]
-                for u in range(f, f + n):
-                    plan.append(("fin", u))
+                fins.extend(range(f, f + n))
+        for i in range(fins_a_step if k < n_tiles else n_tiles):
+            if st["fin"] < len(fins):
+                plan.append(("fin", fins[st["fin"]]))
+                st["fin"] += 1
+        k += 1
     return plan
 
 
@@ -93,11 +106,11 @@ def spans(sizes):
     return out
 
 
-GROUPS = spans([1, 1] + [2] * 31)
+GROUPS = spans([1] * 6 + [2] * 29)
 VECTOR_TILES = (22, 24, 38, 40, 52, 54)
 MODES = [("G" if f in VECTOR_TILES else "P") for (f, n) in GROUPS]
 BATCHES = spans([8] * 7 + [4, 4])
-LOOK = (8, 6, 4, 3, 1, 2)
+LOOK = (8, 6, 4, 3, 2)
 FIN_VECTOR_FROM = 60
 
 
@@ -106,7 +119,7 @@ def tile_transducer_kernel(tc, enc_state, dec_state, W1, b1, W2, b2, out):
     enc2 = enc_state.flatten_outer_dims()
     dec2 = dec_state.flatten_outer_dims()
     outf = out.flatten_outer_dims()
-    plan = make_plan(GROUPS, MODES, BATCHES, LOOK, 8)
+    plan = make_plan(GROUPS, MODES, BATCHES, LOOK, 2, 8, 2)
     group_of = {}
     for g, (f, n) in enumerate(GROUPS):
         for t in range(f, f + n):
@@ -136,8 +149,9 @@ def tile_transducer_kernel(tc, enc_state, dec_state, W1, b1, W2, b2, out):
                 out=raw1[:, a].rearrange("p (u e) c -> p u e c", u=2),
                 in_=W1[a * 512 : (a + 1) * 512, :].rearrange("(u q e) c -> q u e c", u=2, e=2),
             )
-        raw2 = const.tile([P, 4, 1024], BF16, name="raw2")
-        nc.sync.dma_start(out=raw2[:], in_=W2.rearrange("(p j) v -> p j v", j=4))
+        raw2 = const.tile([P, 2, 4, 512], BF16, name="raw2")
+        for h in range(2):
+            nc.sync.dma_start(out=raw2[:, h], in_=W2[:, h * 512 : (h + 1) * 512].rearrange("(p j) v -> p j v", j=4))
         b2_bc = const.tile([P, 1024], BF16, name="b2_bc")
         nc.sync.dma_start(out=b2_bc[:], in_=b2.partition_broadcast(P))
 
@@ -145,13 +159,17 @@ def tile_transducer_kernel(tc, enc_state, dec_state, W1, b1, W2, b2, out):
         masks.make_identity(nc, ident[:])
         xg = const.tile([P, 4096], BF16, name="xg", align_bytes=64)
         nc.gpsimd.memset(xg[:].bitcast(F32), 0.0)
-        b1row = const.tile([P, 512], F32, name="b1row")
-        nc.gpsimd.memset(b1row[:], 0.0)
+        pmat = const.tile([P, 4, 512], F32, name="pmat")
+        nc.gpsimd.memset(pmat[96:128, :, :], 0.0)
 
         warm = const.tile([P, 1], F32, name="warm")
         nc.vector.memset(warm[:], 0.0)
         warm2 = const.tile([P, 1], F32, name="warm2")
         nc.scalar.activation(out=warm2[:], in_=warm[:], func=ACT.Exp)
+        nc.scalar.copy(
+            out=pmat[96:97, :, :].rearrange("o b (j m) -> o b j m", j=4),
+            in_=b1_st[96:97, :].rearrange("o (m j) -> o j m", j=4).unsqueeze(1).to_broadcast([1, 4, 4, P]),
+        )
 
         sel = const.tile([P, 2048], F32, name="sel")
         nc.vector.scalar_tensor_tensor(
@@ -161,10 +179,6 @@ def tile_transducer_kernel(tc, enc_state, dec_state, W1, b1, W2, b2, out):
             in1=ident[:, 64:96].unsqueeze(1).to_broadcast([P, 64, 32]),
             op0=ALU.add,
             op1=ALU.add,
-        )
-        nc.vector.tensor_copy(
-            out=b1row[96:97, :].rearrange("o (j m) -> o j m", j=4),
-            in_=b1_st[96:97, :].rearrange("o (m j) -> o j m", j=4),
         )
 
         xt_e = ps.tile([P, 512], F32, tag="lg", name="xt_e")
@@ -204,22 +218,28 @@ def tile_transducer_kernel(tc, enc_state, dec_state, W1, b1, W2, b2, out):
         g1 = const.tile([P, 2, 2048], BF16, name="g1", align_bytes=64)
         w1c = const.tile([P, 1024], U32, name="w1c", align_bytes=64)
         w1s = const.tile([P, 1024], U8, name="w1s", align_bytes=64)
-        nc.vector.tensor_copy(
-            out=g1[:, 0, :].rearrange("p (j m t) -> p j m t", j=4, t=4),
-            in_=raw1[:, 0].rearrange("p t (m j) -> p j m t", j=4),
-        )
-        nc.scalar.copy(
-            out=g1[:, 1, :].rearrange("p (j m t) -> p j m t", j=4, t=4),
-            in_=raw1[:, 1].rearrange("p t (m j) -> p j m t", j=4),
-        )
-        for a in range(2):
+
+        def w1_views(a, j0, j1):
+            dst = g1[:, a, :].rearrange("p (j m t) -> p j m t", j=4, t=4)[:, j0:j1]
+            src = raw1[:, a].rearrange("p t (m j) -> p j m t", j=4)[:, j0:j1]
+            return dst, src
+
+        def quant_w1(a):
             nc.vector.quantize_mx(
                 out=w1c[:, a * 512 : (a + 1) * 512].bitcast(FP8X4),
                 scales=w1s[:, a * 512 : (a + 1) * 512],
                 in_=g1[:, a, :],
             )
 
-        pmat = const.tile([P, 4, 512], F32, name="pmat")
+        dst, src = w1_views(0, 0, 4)
+        nc.vector.tensor_copy(out=dst, in_=src)
+        quant_w1(0)
+        dst, src = w1_views(1, 2, 4)
+        nc.scalar.copy(out=dst, in_=src)
+        dst, src = w1_views(1, 0, 2)
+        nc.vector.tensor_copy(out=dst, in_=src)
+        quant_w1(1)
+
         pp = []
         for b in range(4):
             acc = ps.tile([P, 512], F32, tag="lg", name="pp%d" % b)
@@ -235,24 +255,33 @@ def tile_transducer_kernel(tc, enc_state, dec_state, W1, b1, W2, b2, out):
                     start=(a == 0),
                     stop=(a == 1),
                 )
-        nc.vector.tensor_tensor(out=pmat[:, 0, :], in0=pp[0][:], in1=b1row[:], op=ALU.add)
+        nc.vector.tensor_copy(out=pmat[0:96, 0, :], in_=pp[0][0:96, :])
+        for b in range(1, 4):
+            nc.scalar.copy(out=pmat[0:96, b, :], in_=pp[b][0:96, :])
 
         g2 = const.tile([P, 4096], BF16, name="g2", align_bytes=64)
         w2c = const.tile([P, 1024], U32, name="w2c", align_bytes=64)
         w2s = const.tile([P, 1024], U8, name="w2s", align_bytes=64)
         nc.vector.tensor_copy(
             out=g2[:, 0:2048].rearrange("p (v j) -> p v j", j=4),
-            in_=raw2[:, :, 0:512].rearrange("p j v -> p v j"),
+            in_=raw2[:, 0].rearrange("p j v -> p v j"),
         )
-        nc.scalar.copy(
+        nc.gpsimd.tensor_scalar(
             out=g2[:, 2048:4096].rearrange("p (v j) -> p v j", j=4),
-            in_=raw2[:, :, 512:1024].rearrange("p j v -> p v j"),
+            in0=raw2[:, 1].rearrange("p j v -> p v j"),
+            scalar1=1.0,
+            scalar2=0.0,
+            op0=ALU.mult,
+            op1=ALU.add,
         )
-        nc.vector.quantize_mx(out=w2c[:].bitcast(FP8X4), scales=w2s[:], in_=g2[:])
+        for h in range(2):
+            nc.vector.quantize_mx(
+                out=w2c[:, h * 512 : (h + 1) * 512].bitcast(FP8X4),
+                scales=w2s[:, h * 512 : (h + 1) * 512],
+                in_=g2[:, h * 2048 : (h + 1) * 2048],
+            )
         b2f = const.tile([P, 1024], F32, name="b2f")
         nc.gpsimd.tensor_scalar(out=b2f[:], in0=b2_bc[:], scalar1=1.0, scalar2=0.0, op0=ALU.mult, op1=ALU.add)
-        for b in range(1, 4):
-            nc.vector.tensor_tensor(out=pmat[:, b, :], in0=pp[b][:], in1=b1row[:], op=ALU.add)
 
         ed = {}
         pbank = {}

@@ -17,8 +17,8 @@ P = 128
 FLOPS = 2 * (256 * 512 * 512 + 128 * 512 * 512 + 8192 * 512 * 1024)
 
 
-def make_plan(groups, modes, batches, look, start, prep_lead, fins_a_step):
-    look_add, look_tanh, look_quant, look_mx, lag_exp = look
+def make_plan(groups, modes, batches, look, prep_lead):
+    look_add, look_tanh, look_quant, look_mx, lag_red, lag_exp = look
     n_groups = len(groups)
     n_tiles = sum(n for (f, n) in groups)
     group_of = {}
@@ -35,18 +35,9 @@ def make_plan(groups, modes, batches, look, start, prep_lead, fins_a_step):
             prepared.add(f // 16)
             prep_at[max(f - prep_lead, 0)] = f // 16
     plan = []
-    for t in range(start):
-        plan.append(("padd", t))
-        plan.append(("ptanh", t))
-        if t >= 1:
-            plan.append(("quant", t - 1))
-            plan.append(("mx", t - 1))
-    st = {"add": start, "tanh": start, "quant": start - 1, "mx": start - 1, "exp": 0, "fin": 0}
-    fins = []
-    k = 0
-    while st["fin"] < n_tiles:
-        less = max(0, look_add - start - (k + 1) // 2)
-        while st["add"] < n_tiles and st["add"] <= k + look_add - less:
+    st = {"add": 0, "tanh": 0, "quant": 0, "mx": 0}
+    for k in range(-look_add, n_tiles + lag_exp + 1):
+        while st["add"] < n_tiles and st["add"] <= k + look_add:
             t = st["add"]
             g = group_of[t]
             if t in prep_at:
@@ -56,7 +47,7 @@ def make_plan(groups, modes, batches, look, start, prep_lead, fins_a_step):
             elif t == groups[g][0]:
                 plan.append(("add", g))
             st["add"] += 1
-        while st["tanh"] < st["add"] and st["tanh"] <= k + look_tanh - less:
+        while st["tanh"] < st["add"] and st["tanh"] <= k + look_tanh:
             t = st["tanh"]
             g = group_of[t]
             if modes[g] == "P":
@@ -66,7 +57,7 @@ def make_plan(groups, modes, batches, look, start, prep_lead, fins_a_step):
             st["tanh"] += 1
         while st["quant"] < n_groups:
             f, n = groups[st["quant"]]
-            if f + n - 1 < st["tanh"] and f + n - 1 <= k + max(look_quant - less, 1):
+            if f + n - 1 < st["tanh"] and f + n - 1 <= k + look_quant:
                 plan.append(("quant", st["quant"]))
                 st["quant"] += 1
             else:
@@ -74,26 +65,21 @@ def make_plan(groups, modes, batches, look, start, prep_lead, fins_a_step):
         while st["mx"] < n_tiles and st["mx"] <= k + look_mx and group_of[st["mx"]] < st["quant"]:
             plan.append(("mx", st["mx"]))
             st["mx"] += 1
-        if k < n_tiles:
+        if 0 <= k < n_tiles:
             assert st["mx"] > k, (k, st)
             plan.append(("ev", k, 0))
             plan.append(("ev", k, 1))
-        if 0 <= k - 1 < n_tiles:
-            plan.append(("red", k - 1))
-        while st["exp"] < min(k, n_tiles) and (st["exp"] <= k - lag_exp or k >= n_tiles):
-            t = st["exp"]
+        if 0 <= k - lag_red < n_tiles:
+            plan.append(("red", k - lag_red))
+        t = k - lag_exp
+        if 0 <= t < n_tiles:
             plan.append(("exp", t))
-            st["exp"] += 1
             if t in last_b:
                 b = last_b[t]
                 plan.append(("ln", b))
                 f, n = batches[b]
-                fins.extend(range(f, f + n))
-        for i in range(fins_a_step if k < n_tiles else n_tiles):
-            if st["fin"] < len(fins):
-                plan.append(("fin", fins[st["fin"]]))
-                st["fin"] += 1
-        k += 1
+                for u in range(f, f + n):
+                    plan.append(("fin", u))
     return plan
 
 
@@ -106,12 +92,12 @@ def spans(sizes):
     return out
 
 
-GROUPS = spans([1] * 6 + [2] * 29)
+GROUPS = spans([1, 1] + [2] * 31)
 VECTOR_TILES = (22, 24, 38, 40, 52, 54)
 MODES = [("G" if f in VECTOR_TILES else "P") for (f, n) in GROUPS]
-BATCHES = spans([8] * 7 + [4, 4])
-LOOK = (8, 6, 4, 3, 2)
-FIN_VECTOR_FROM = 60
+BATCHES = spans([16] * 3 + [8, 4, 4])
+LOOK = (8, 6, 4, 3, 1, 2)
+LAST_FINS = {60: "V", 61: "S", 62: "G", 63: "V"}
 
 
 def tile_transducer_kernel(tc, enc_state, dec_state, W1, b1, W2, b2, out):
@@ -119,7 +105,7 @@ def tile_transducer_kernel(tc, enc_state, dec_state, W1, b1, W2, b2, out):
     enc2 = enc_state.flatten_outer_dims()
     dec2 = dec_state.flatten_outer_dims()
     outf = out.flatten_outer_dims()
-    plan = make_plan(GROUPS, MODES, BATCHES, LOOK, 2, 8, 2)
+    plan = make_plan(GROUPS, MODES, BATCHES, LOOK, 8)
     group_of = {}
     for g, (f, n) in enumerate(GROUPS):
         for t in range(f, f + n):
@@ -132,8 +118,8 @@ def tile_transducer_kernel(tc, enc_state, dec_state, W1, b1, W2, b2, out):
     with ExitStack() as ctx:
         const = ctx.enter_context(tc.tile_pool(name="const", bufs=1))
         work = ctx.enter_context(tc.tile_pool(name="work", bufs=3))
-        zpool = ctx.enter_context(tc.tile_pool(name="zpool", bufs=24))
-        small = ctx.enter_context(tc.tile_pool(name="small", bufs=9))
+        zpool = ctx.enter_context(tc.tile_pool(name="zpool", bufs=30))
+        small = ctx.enter_context(tc.tile_pool(name="small", bufs=6))
         ps = ctx.enter_context(tc.psum_pool(name="ps", bufs=6))
         ctx.enter_context(tc.manual_schedule())
 
@@ -141,6 +127,7 @@ def tile_transducer_kernel(tc, enc_state, dec_state, W1, b1, W2, b2, out):
         nc.sync.dma_start(out=enc_sb[:], in_=enc2.rearrange("(s p) h -> p s h", p=P))
         dec_sb = const.tile([P, 512], BF16, name="dec_sb")
         nc.sync.dma_start(out=dec_sb[:], in_=dec2)
+        b2_bc = const.tile([P, 1024], BF16, name="b2_bc")
         b1_st = const.tile([P, 512], BF16, name="b1_st")
         nc.sync.dma_start(out=b1_st[96:97, :], in_=b1.rearrange("(o c) -> o c", o=1))
         raw1 = const.tile([P, 2, 4, 512], BF16, name="raw1")
@@ -149,27 +136,21 @@ def tile_transducer_kernel(tc, enc_state, dec_state, W1, b1, W2, b2, out):
                 out=raw1[:, a].rearrange("p (u e) c -> p u e c", u=2),
                 in_=W1[a * 512 : (a + 1) * 512, :].rearrange("(u q e) c -> q u e c", u=2, e=2),
             )
-        raw2 = const.tile([P, 2, 4, 512], BF16, name="raw2")
-        for h in range(2):
-            nc.sync.dma_start(out=raw2[:, h], in_=W2[:, h * 512 : (h + 1) * 512].rearrange("(p j) v -> p j v", j=4))
-        b2_bc = const.tile([P, 1024], BF16, name="b2_bc")
         nc.sync.dma_start(out=b2_bc[:], in_=b2.partition_broadcast(P))
+        raw2 = const.tile([P, 4, 1024], BF16, name="raw2")
+        nc.sync.dma_start(out=raw2[:], in_=W2.rearrange("(p j) v -> p j v", j=4))
 
         ident = const.tile([P, P], F32, name="ident")
         masks.make_identity(nc, ident[:])
         xg = const.tile([P, 4096], BF16, name="xg", align_bytes=64)
         nc.gpsimd.memset(xg[:].bitcast(F32), 0.0)
-        pmat = const.tile([P, 4, 512], F32, name="pmat")
-        nc.gpsimd.memset(pmat[96:128, :, :], 0.0)
+        b1row = const.tile([P, 512], F32, name="b1row")
+        nc.gpsimd.memset(b1row[:], 0.0)
 
         warm = const.tile([P, 1], F32, name="warm")
         nc.vector.memset(warm[:], 0.0)
         warm2 = const.tile([P, 1], F32, name="warm2")
         nc.scalar.activation(out=warm2[:], in_=warm[:], func=ACT.Exp)
-        nc.scalar.copy(
-            out=pmat[96:97, :, :].rearrange("o b (j m) -> o b j m", j=4),
-            in_=b1_st[96:97, :].rearrange("o (m j) -> o j m", j=4).unsqueeze(1).to_broadcast([1, 4, 4, P]),
-        )
 
         sel = const.tile([P, 2048], F32, name="sel")
         nc.vector.scalar_tensor_tensor(
@@ -179,6 +160,10 @@ def tile_transducer_kernel(tc, enc_state, dec_state, W1, b1, W2, b2, out):
             in1=ident[:, 64:96].unsqueeze(1).to_broadcast([P, 64, 32]),
             op0=ALU.add,
             op1=ALU.add,
+        )
+        nc.vector.tensor_copy(
+            out=b1row[96:97, :].rearrange("o (j m) -> o j m", j=4),
+            in_=b1_st[96:97, :].rearrange("o (m j) -> o j m", j=4),
         )
 
         xt_e = ps.tile([P, 512], F32, tag="lg", name="xt_e")
@@ -218,28 +203,22 @@ def tile_transducer_kernel(tc, enc_state, dec_state, W1, b1, W2, b2, out):
         g1 = const.tile([P, 2, 2048], BF16, name="g1", align_bytes=64)
         w1c = const.tile([P, 1024], U32, name="w1c", align_bytes=64)
         w1s = const.tile([P, 1024], U8, name="w1s", align_bytes=64)
-
-        def w1_views(a, j0, j1):
-            dst = g1[:, a, :].rearrange("p (j m t) -> p j m t", j=4, t=4)[:, j0:j1]
-            src = raw1[:, a].rearrange("p t (m j) -> p j m t", j=4)[:, j0:j1]
-            return dst, src
-
-        def quant_w1(a):
+        nc.vector.tensor_copy(
+            out=g1[:, 0, :].rearrange("p (j m t) -> p j m t", j=4, t=4),
+            in_=raw1[:, 0].rearrange("p t (m j) -> p j m t", j=4),
+        )
+        nc.scalar.copy(
+            out=g1[:, 1, :].rearrange("p (j m t) -> p j m t", j=4, t=4),
+            in_=raw1[:, 1].rearrange("p t (m j) -> p j m t", j=4),
+        )
+        for a in range(2):
             nc.vector.quantize_mx(
                 out=w1c[:, a * 512 : (a + 1) * 512].bitcast(FP8X4),
                 scales=w1s[:, a * 512 : (a + 1) * 512],
                 in_=g1[:, a, :],
             )
 
-        dst, src = w1_views(0, 0, 4)
-        nc.vector.tensor_copy(out=dst, in_=src)
-        quant_w1(0)
-        dst, src = w1_views(1, 2, 4)
-        nc.scalar.copy(out=dst, in_=src)
-        dst, src = w1_views(1, 0, 2)
-        nc.vector.tensor_copy(out=dst, in_=src)
-        quant_w1(1)
-
+        pmat = const.tile([P, 4, 512], F32, name="pmat")
         pp = []
         for b in range(4):
             acc = ps.tile([P, 512], F32, tag="lg", name="pp%d" % b)
@@ -255,33 +234,22 @@ def tile_transducer_kernel(tc, enc_state, dec_state, W1, b1, W2, b2, out):
                     start=(a == 0),
                     stop=(a == 1),
                 )
-        nc.vector.tensor_copy(out=pmat[0:96, 0, :], in_=pp[0][0:96, :])
-        for b in range(1, 4):
-            nc.scalar.copy(out=pmat[0:96, b, :], in_=pp[b][0:96, :])
+        nc.vector.tensor_tensor(out=pmat[:, 0, :], in0=pp[0][:], in1=b1row[:], op=ALU.add)
 
         g2 = const.tile([P, 4096], BF16, name="g2", align_bytes=64)
         w2c = const.tile([P, 1024], U32, name="w2c", align_bytes=64)
         w2s = const.tile([P, 1024], U8, name="w2s", align_bytes=64)
         nc.vector.tensor_copy(
             out=g2[:, 0:2048].rearrange("p (v j) -> p v j", j=4),
-            in_=raw2[:, 0].rearrange("p j v -> p v j"),
+            in_=raw2[:, :, 0:512].rearrange("p j v -> p v j"),
         )
-        nc.gpsimd.tensor_scalar(
+        nc.scalar.copy(
             out=g2[:, 2048:4096].rearrange("p (v j) -> p v j", j=4),
-            in0=raw2[:, 1].rearrange("p j v -> p v j"),
-            scalar1=1.0,
-            scalar2=0.0,
-            op0=ALU.mult,
-            op1=ALU.add,
+            in_=raw2[:, :, 512:1024].rearrange("p j v -> p v j"),
         )
-        for h in range(2):
-            nc.vector.quantize_mx(
-                out=w2c[:, h * 512 : (h + 1) * 512].bitcast(FP8X4),
-                scales=w2s[:, h * 512 : (h + 1) * 512],
-                in_=g2[:, h * 2048 : (h + 1) * 2048],
-            )
-        b2f = const.tile([P, 1024], F32, name="b2f")
-        nc.gpsimd.tensor_scalar(out=b2f[:], in0=b2_bc[:], scalar1=1.0, scalar2=0.0, op0=ALU.mult, op1=ALU.add)
+        nc.vector.quantize_mx(out=w2c[:].bitcast(FP8X4), scales=w2s[:], in_=g2[:])
+        for b in range(1, 4):
+            nc.vector.tensor_tensor(out=pmat[:, b, :], in0=pp[b][:], in1=b1row[:], op=ALU.add)
 
         ed = {}
         pbank = {}
@@ -297,7 +265,7 @@ def tile_transducer_kernel(tc, enc_state, dec_state, W1, b1, W2, b2, out):
             if b not in bt:
                 d = {}
                 for nm in ("negm", "ssum", "lns", "negc"):
-                    d[nm] = small.tile([P, 8], F32, tag=nm, name="%s%d" % (nm, b))
+                    d[nm] = small.tile([P, 16], F32, tag=nm, name="%s%d" % (nm, b))
                 bt[b] = d
             return bt[b]
 
@@ -380,7 +348,7 @@ def tile_transducer_kernel(tc, enc_state, dec_state, W1, b1, W2, b2, out):
                 t, h = op[1], op[2]
                 if h == 0:
                     zt[t] = zpool.tile([P, 1024], F32, tag="z", name="z%d" % t)
-                nc.vector.tensor_tensor(out=zt[t][:, h * 512 : (h + 1) * 512], in0=lg[(t, h)][:], in1=b2f[:, h * 512 : (h + 1) * 512], op=ALU.add)
+                nc.vector.tensor_tensor(out=zt[t][:, h * 512 : (h + 1) * 512], in0=lg[(t, h)][:], in1=b2_bc[:, h * 512 : (h + 1) * 512], op=ALU.add)
             elif kind == "red":
                 t = op[1]
                 b = batch_of[t]
@@ -398,14 +366,18 @@ def tile_transducer_kernel(tc, enc_state, dec_state, W1, b1, W2, b2, out):
                 n = BATCHES[b][1]
                 d = batch_tiles(b)
                 nc.scalar.activation(out=d["lns"][:, :n], in_=d["ssum"][:, :n], func=ACT.Ln)
-                nc.gpsimd.tensor_tensor(out=d["negc"][:, :n], in0=d["negm"][:, :n], in1=d["lns"][:, :n], op=ALU.subtract)
+                eng = nc.vector if b == len(BATCHES) - 1 else nc.gpsimd
+                eng.tensor_tensor(out=d["negc"][:, :n], in0=d["negm"][:, :n], in1=d["lns"][:, :n], op=ALU.subtract)
             else:
                 t = op[1]
                 b = batch_of[t]
                 c = t - BATCHES[b][0]
                 negc = batch_tiles(b)["negc"][:, c : c + 1]
-                if t >= FIN_VECTOR_FROM:
+                who = LAST_FINS.get(t, "G")
+                if who == "V":
                     nc.vector.tensor_scalar(out=zt[t][:], in0=zt[t][:], scalar1=negc, scalar2=None, op0=ALU.add)
+                elif who == "S":
+                    nc.scalar.activation(out=zt[t][:], in_=zt[t][:], func=ACT.Identity, bias=negc, scale=1.0)
                 else:
                     nc.gpsimd.tensor_scalar(out=zt[t][:], in0=zt[t][:], scalar1=1.0, scalar2=negc, op0=ALU.mult, op1=ALU.add)
                 nc.sync.dma_start(out=outf[t * P : (t + 1) * P, :], in_=zt[t][:])

@@ -121,7 +121,7 @@ def tile_transducer_kernel(tc, enc_state, dec_state, W1, b1, W2, b2, out):
         zpool = ctx.enter_context(tc.tile_pool(name="zpool", bufs=30))
         small = ctx.enter_context(tc.tile_pool(name="small", bufs=6))
         ps = ctx.enter_context(tc.psum_pool(name="ps", bufs=6))
-        ctx.enter_context(tc.manual_schedule())
+        pass
 
         enc_sb = const.tile([P, 2, 512], BF16, name="enc_sb")
         nc.sync.dma_start(out=enc_sb[:], in_=enc2.rearrange("(s p) h -> p s h", p=P))

@@ -17,7 +17,7 @@ P = 128
 FLOPS = 2 * (256 * 512 * 512 + 128 * 512 * 512 + 8192 * 512 * 1024)
 
 
-def make_plan(groups, modes, batches, look, prep_lead):
+def make_plan(groups, modes, batches, look, prep_lead, room):
     look_add, look_tanh, look_quant, look_mx, lag_red, lag_exp = look
     n_groups = len(groups)
     n_tiles = sum(n for (f, n) in groups)
@@ -35,7 +35,24 @@ def make_plan(groups, modes, batches, look, prep_lead):
             prepared.add(f // 16)
             prep_at[max(f - prep_lead, 0)] = f // 16
     plan = []
-    st = {"add": 0, "tanh": 0, "quant": 0, "mx": 0}
+    st = {"add": 0, "tanh": 0, "quant": 0, "mx": 0, "fin": 0, "used": 0}
+    fins = []
+    waiting = []
+
+    def sums():
+        while st["used"] < len(waiting):
+            plan.append(("add", waiting[st["used"]]))
+            st["used"] += 1
+
+    def release(n):
+        first = st["fin"]
+        while st["fin"] < len(fins) and st["fin"] - first < n and fins[st["fin"]][0] == fins[first][0]:
+            st["fin"] += 1
+        if st["fin"] > first:
+            plan.append(("negc", fins[first][0], fins[first][1], st["fin"] - first))
+            for i in range(first, st["fin"]):
+                plan.append(("fin", fins[i][1]))
+
     for k in range(-look_add, n_tiles + lag_exp + 1):
         while st["add"] < n_tiles and st["add"] <= k + look_add:
             t = st["add"]
@@ -45,7 +62,7 @@ def make_plan(groups, modes, batches, look, prep_lead):
             if modes[g] == "P":
                 plan.append(("padd", t))
             elif t == groups[g][0]:
-                plan.append(("add", g))
+                waiting.append(g)
             st["add"] += 1
         while st["tanh"] < st["add"] and st["tanh"] <= k + look_tanh:
             t = st["tanh"]
@@ -53,6 +70,7 @@ def make_plan(groups, modes, batches, look, prep_lead):
             if modes[g] == "P":
                 plan.append(("ptanh", t))
             elif t == groups[g][0]:
+                sums()
                 plan.append(("tanh", g))
             st["tanh"] += 1
         while st["quant"] < n_groups:
@@ -60,6 +78,8 @@ def make_plan(groups, modes, batches, look, prep_lead):
             if f + n - 1 < st["tanh"] and f + n - 1 <= k + look_quant:
                 plan.append(("quant", st["quant"]))
                 st["quant"] += 1
+                release(max(room - 2 * (len(waiting) - st["used"]), 1))
+                sums()
             else:
                 break
         while st["mx"] < n_tiles and st["mx"] <= k + look_mx and group_of[st["mx"]] < st["quant"]:
@@ -79,7 +99,11 @@ def make_plan(groups, modes, batches, look, prep_lead):
                 plan.append(("ln", b))
                 f, n = batches[b]
                 for u in range(f, f + n):
-                    plan.append(("fin", u))
+                    fins.append((b, u))
+        if st["quant"] == n_groups:
+            release(n_tiles)
+    while st["fin"] < len(fins):
+        release(n_tiles)
     return plan
 
 
@@ -93,11 +117,11 @@ def spans(sizes):
 
 
 GROUPS = spans([1, 1] + [2] * 31)
-VECTOR_TILES = (22, 24, 38, 40, 52, 54)
+VECTOR_TILES = (24, 30, 36, 42, 48, 54)
 MODES = [("G" if f in VECTOR_TILES else "P") for (f, n) in GROUPS]
-BATCHES = spans([16] * 3 + [8, 4, 4])
+BATCHES = spans([12] * 4 + [8, 4, 4])
 LOOK = (8, 6, 4, 3, 1, 2)
-LAST_FINS = {60: "V", 61: "S", 62: "G", 63: "V"}
+LAST_FINS = {60: "V", 61: "S", 62: "V", 63: "S"}
 
 
 def tile_transducer_kernel(tc, enc_state, dec_state, W1, b1, W2, b2, out):
@@ -105,7 +129,7 @@ def tile_transducer_kernel(tc, enc_state, dec_state, W1, b1, W2, b2, out):
     enc2 = enc_state.flatten_outer_dims()
     dec2 = dec_state.flatten_outer_dims()
     outf = out.flatten_outer_dims()
-    plan = make_plan(GROUPS, MODES, BATCHES, LOOK, 8)
+    plan = make_plan(GROUPS, MODES, BATCHES, LOOK, 8, 3)
     group_of = {}
     for g, (f, n) in enumerate(GROUPS):
         for t in range(f, f + n):
@@ -119,9 +143,9 @@ def tile_transducer_kernel(tc, enc_state, dec_state, W1, b1, W2, b2, out):
         const = ctx.enter_context(tc.tile_pool(name="const", bufs=1))
         work = ctx.enter_context(tc.tile_pool(name="work", bufs=3))
         zpool = ctx.enter_context(tc.tile_pool(name="zpool", bufs=30))
-        small = ctx.enter_context(tc.tile_pool(name="small", bufs=6))
+        small = ctx.enter_context(tc.tile_pool(name="small", bufs=7))
         ps = ctx.enter_context(tc.psum_pool(name="ps", bufs=6))
-        pass
+        ctx.enter_context(tc.manual_schedule())
 
         enc_sb = const.tile([P, 2, 512], BF16, name="enc_sb")
         nc.sync.dma_start(out=enc_sb[:], in_=enc2.rearrange("(s p) h -> p s h", p=P))
@@ -366,8 +390,11 @@ def tile_transducer_kernel(tc, enc_state, dec_state, W1, b1, W2, b2, out):
                 n = BATCHES[b][1]
                 d = batch_tiles(b)
                 nc.scalar.activation(out=d["lns"][:, :n], in_=d["ssum"][:, :n], func=ACT.Ln)
-                eng = nc.vector if b == len(BATCHES) - 1 else nc.gpsimd
-                eng.tensor_tensor(out=d["negc"][:, :n], in0=d["negm"][:, :n], in1=d["lns"][:, :n], op=ALU.subtract)
+            elif kind == "negc":
+                b, t, n = op[1], op[2], op[3]
+                c = t - BATCHES[b][0]
+                d = batch_tiles(b)
+                nc.vector.tensor_tensor(out=d["negc"][:, c : c + n], in0=d["negm"][:, c : c + n], in1=d["lns"][:, c : c + n], op=ALU.subtract)
             else:
                 t = op[1]
                 b = batch_of[t]

from contextlib import ExitStack

import concourse.masks as masks
import concourse.mybir as mybir

F32 = mybir.dt.float32
BF16 = mybir.dt.bfloat16
U32 = mybir.dt.uint32
U8 = mybir.dt.uint8
I32 = mybir.dt.int32
FP8X4 = mybir.dt.float8_e4m3fn_x4
ALU = mybir.AluOpType
ACT = mybir.ActivationFunctionType
AX = mybir.AxisListType

P = 128
FLOPS = 2 * (256 * 512 * 512 + 128 * 512 * 512 + 8192 * 512 * 1024)


def make_plan(groups, modes, batches, look, prep_lead, room):
    look_add, look_tanh, look_quant, look_mx, lag_red, lag_exp = look
    n_groups = len(groups)
    n_tiles = sum(n for (f, n) in groups)
    group_of = {}
    for g, (f, n) in enumerate(groups):
        for t in range(f, f + n):
            group_of[t] = g
    last_b = {}
    for b, (f, n) in enumerate(batches):
        last_b[f + n - 1] = b
    prep_at = {}
    prepared = set()
    for g, (f, n) in enumerate(groups):
        if modes[g] != "P" and (f // 16) not in prepared:
            prepared.add(f // 16)
            prep_at[max(f - prep_lead, 0)] = f // 16
    plan = []
    st = {"add": 0, "tanh": 0, "quant": 0, "mx": 0, "fin": 0, "used": 0}
    fins = []
    waiting = []

    def sums():
        while st["used"] < len(waiting):
            plan.append(("add", waiting[st["used"]]))
            st["used"] += 1

    def release(n):
        first = st["fin"]
        while st["fin"] < len(fins) and st["fin"] - first < n and fins[st["fin"]][0] == fins[first][0]:
            st["fin"] += 1
        if st["fin"] > first:
            plan.append(("negc", fins[first][0], fins[first][1], st["fin"] - first))
            for i in range(first, st["fin"]):
                plan.append(("fin", fins[i][1]))

    for k in range(-look_add, n_tiles + lag_exp + 1):
        while st["add"] < n_tiles and st["add"] <= k + look_add:
            t = st["add"]
            g = group_of[t]
            if t in prep_at:
                plan.append(("prep", prep_at[t]))
            if modes[g] == "P":
                plan.append(("padd", t))
            elif t == groups[g][0]:
                waiting.append(g)
            st["add"] += 1
        while st["tanh"] < st["add"] and st["tanh"] <= k + look_tanh:
            t = st["tanh"]
            g = group_of[t]
            if modes[g] == "P":
                plan.append(("ptanh", t))
            elif t == groups[g][0]:
                sums()
                plan.append(("tanh", g))
            st["tanh"] += 1
        while st["quant"] < n_groups:
            f, n = groups[st["quant"]]
            if f + n - 1 < st["tanh"] and f + n - 1 <= k + look_quant:
                plan.append(("quant", st["quant"]))
                st["quant"] += 1
                release(max(room - 2 * (len(waiting) - st["used"]), 1))
                sums()
            else:
                break
        while st["mx"] < n_tiles and st["mx"] <= k + look_mx and group_of[st["mx"]] < st["quant"]:
            plan.append(("mx", st["mx"]))
            st["mx"] += 1
        if 0 <= k < n_tiles:
            assert st["mx"] > k, (k, st)
            plan.append(("ev", k, 0))
            plan.append(("ev", k, 1))
        if 0 <= k - lag_red < n_tiles:
            plan.append(("red", k - lag_red))
        t = k - lag_exp
        if 0 <= t < n_tiles:
            plan.append(("exp", t))
            if t in last_b:
                b = last_b[t]
                plan.append(("ln", b))
                f, n = batches[b]
                for u in range(f, f + n):
                    fins.append((b, u))
        if st["quant"] == n_groups:
            release(n_tiles)
    while st["fin"] < len(fins):
        release(n_tiles)
    return plan


def spans(sizes):
    out = []
    f = 0
    for n in sizes:
        out.append((f, n))
        f += n
    return out


GROUPS = spans([1, 1] + [2] * 31)
VECTOR_TILES = (24, 30, 36, 42, 48, 54)
MODES = [("G" if f in VECTOR_TILES else "P") for (f, n) in GROUPS]
BATCHES = spans([12] * 4 + [8, 4, 4])
LOOK = (8, 6, 4, 3, 1, 2)
LAST_FINS = {60: "V", 61: "S", 62: "V", 63: "S"}


def tile_transducer_kernel(tc, enc_state, dec_state, W1, b1, W2, b2, out):
    nc = tc.nc
    enc2 = enc_state.flatten_outer_dims()
    dec2 = dec_state.flatten_outer_dims()
    outf = out.flatten_outer_dims()
    plan = make_plan(GROUPS, MODES, BATCHES, LOOK, 8, 3)
    group_of = {}
    for g, (f, n) in enumerate(GROUPS):
        for t in range(f, f + n):
            group_of[t] = g
    batch_of = {}
    for b, (f, n) in enumerate(BATCHES):
        for t in range(f, f + n):
            batch_of[t] = b

    with ExitStack() as ctx:
        const = ctx.enter_context(tc.tile_pool(name="const", bufs=1))
        work = ctx.enter_context(tc.tile_pool(name="work", bufs=3))
        zpool = ctx.enter_context(tc.tile_pool(name="zpool", bufs=30))
        small = ctx.enter_context(tc.tile_pool(name="small", bufs=7))
        ps = ctx.enter_context(tc.psum_pool(name="ps", bufs=6))
        ctx.enter_context(tc.manual_schedule())

        enc_sb = const.tile([P, 2, 512], BF16, name="enc_sb")
        nc.sync.dma_start(out=enc_sb[:], in_=enc2.rearrange("(s p) h -> p s h", p=P))
        dec_sb = const.tile([P, 512], BF16, name="dec_sb")
        nc.sync.dma_start(out=dec_sb[:], in_=dec2)
        b2_bc = const.tile([P, 1024], BF16, name="b2_bc")
        b1_st = const.tile([P, 512], BF16, name="b1_st")
        nc.sync.dma_start(out=b1_st[96:97, :], in_=b1.rearrange("(o c) -> o c", o=1))
        raw1 = const.tile([P, 2, 4, 512], BF16, name="raw1")
        for a in range(2):
            nc.sync.dma_start(
                out=raw1[:, a].rearrange("p (u e) c -> p u e c", u=2),
                in_=W1[a * 512 : (a + 1) * 512, :].rearrange("(u q e) c -> q u e c", u=2, e=2),
            )
        nc.sync.dma_start(out=b2_bc[:], in_=b2.partition_broadcast(P))
        raw2 = const.tile([P, 4, 1024], BF16, name="raw2")
        nc.sync.dma_start(out=raw2[:], in_=W2.rearrange("(p j) v -> p j v", j=4))

        ident = const.tile([P, P], F32, name="ident")
        masks.make_identity(nc, ident[:])
        xg = const.tile([P, 4096], BF16, name="xg", align_bytes=64)
        nc.gpsimd.memset(xg[:].bitcast(F32), 0.0)
        b1row = const.tile([P, 512], F32, name="b1row")
        nc.gpsimd.memset(b1row[:], 0.0)

        warm = const.tile([P, 1], F32, name="warm")
        nc.vector.memset(warm[:], 0.0)
        warm2 = const.tile([P, 1], F32, name="warm2")
        nc.scalar.activation(out=warm2[:], in_=warm[:], func=ACT.Exp)

        sel = const.tile([P, 2048], F32, name="sel")
        nc.vector.scalar_tensor_tensor(
            out=sel[:].rearrange("p (c u) -> p c u", u=32),
            in0=ident[:, 0:64].unsqueeze(2).to_broadcast([P, 64, 32]),
            scalar=ident[:, 96:97],
            in1=ident[:, 64:96].unsqueeze(1).to_broadcast([P, 64, 32]),
            op0=ALU.add,
            op1=ALU.add,
        )
        nc.vector.tensor_copy(
            out=b1row[96:97, :].rearrange("o (j m) -> o j m", j=4),
            in_=b1_st[96:97, :].rearrange("o (m j) -> o j m", j=4),
        )

        xt_e = ps.tile([P, 512], F32, tag="lg", name="xt_e")
        for s in range(2):
            for u in range(2):
                nc.tensor.transpose(
                    out=xt_e[:, (2 * s + u) * P : (2 * s + u + 1) * P],
                    in_=enc_sb[:, s, :].bitcast(F32)[:, u * P : (u + 1) * P],
                    identity=ident[:],
                )
        xt_d = ps.tile([P, 512], F32, tag="lg", name="xt_d")
        for u in range(2):
            nc.tensor.transpose(
                out=xt_d[:, u * P : (u + 1) * P],
                in_=dec_sb[:].bitcast(F32)[:, u * P : (u + 1) * P],
                identity=ident[:],
            )
        xgf = xg[:].bitcast(F32).rearrange("p (a c u) -> p a c u", a=8, u=2)
        for s in range(2):
            nc.vector.tensor_copy(
                out=xgf[:, 2 * s : 2 * s + 2, 0:64, :],
                in_=xt_e[:, s * 256 : (s + 1) * 256].rearrange("p (u b t) -> p b t u", u=2, b=2),
            )
        nc.vector.tensor_copy(
            out=xgf[:, 4:8, 64:96, :],
            in_=xt_d[:, 0:256].rearrange("p (e b u) -> p b u e", e=2, b=4),
        )
        xc = const.tile([P, 1024], U32, name="xc", align_bytes=64)
        xs = const.tile([P, 1024], U8, name="xs", align_bytes=64)
        for a in range(2):
            nc.vector.quantize_mx(
                out=xc[:, a * 512 : (a + 1) * 512].bitcast(FP8X4),
                scales=xs[:, a * 512 : (a + 1) * 512],
                in_=xg[:, a * 2048 : (a + 1) * 2048],
            )

        g1 = const.tile([P, 2, 2048], BF16, name="g1", align_bytes=64)
        w1c = const.tile([P, 1024], U32, name="w1c", align_bytes=64)
        w1s = const.tile([P, 1024], U8, name="w1s", align_bytes=64)
        nc.vector.tensor_copy(
            out=g1[:, 0, :].rearrange("p (j m t) -> p j m t", j=4, t=4),
            in_=raw1[:, 0].rearrange("p t (m j) -> p j m t", j=4),
        )
        nc.scalar.copy(
            out=g1[:, 1, :].rearrange("p (j m t) -> p j m t", j=4, t=4),
            in_=raw1[:, 1].rearrange("p t (m j) -> p j m t", j=4),
        )
        for a in range(2):
            nc.vector.quantize_mx(
                out=w1c[:, a * 512 : (a + 1) * 512].bitcast(FP8X4),
                scales=w1s[:, a * 512 : (a + 1) * 512],
                in_=g1[:, a, :],
            )

        pmat = const.tile([P, 4, 512], F32, name="pmat")
        pp = []
        for b in range(4):
            acc = ps.tile([P, 512], F32, tag="lg", name="pp%d" % b)
            pp.append(acc)
            for a in range(2):
                o = (4 * a + b) * P
                nc.tensor.matmul_mx(
                    out=acc[:],
                    lhsT=xc[:, o : o + P].bitcast(FP8X4),
                    lhsT_scale=xs[:, o : o + P],
                    rhs=w1c[:, a * 512 : (a + 1) * 512].bitcast(FP8X4),
                    rhs_scale=w1s[:, a * 512 : (a + 1) * 512],
                    start=(a == 0),
                    stop=(a == 1),
                )
        nc.vector.tensor_tensor(out=pmat[:, 0, :], in0=pp[0][:], in1=b1row[:], op=ALU.add)

        g2 = const.tile([P, 4096], BF16, name="g2", align_bytes=64)
        w2c = const.tile([P, 1024], U32, name="w2c", align_bytes=64)
        w2s = const.tile([P, 1024], U8, name="w2s", align_bytes=64)
        nc.vector.tensor_copy(
            out=g2[:, 0:2048].rearrange("p (v j) -> p v j", j=4),
            in_=raw2[:, :, 0:512].rearrange("p j v -> p v j"),
        )
        nc.scalar.copy(
            out=g2[:, 2048:4096].rearrange("p (v j) -> p v j", j=4),
            in_=raw2[:, :, 512:1024].rearrange("p j v -> p v j"),
        )
        nc.vector.quantize_mx(out=w2c[:].bitcast(FP8X4), scales=w2s[:], in_=g2[:])
        for b in range(1, 4):
            nc.vector.tensor_tensor(out=pmat[:, b, :], in0=pp[b][:], in1=b1row[:], op=ALU.add)

        ed = {}
        pbank = {}
        pre = {}
        hid = {}
        hcod = {}
        hsc = {}
        lg = {}
        zt = {}
        bt = {}

        def batch_tiles(b):
            if b not in bt:
                d = {}
                for nm in ("negm", "ssum", "lns", "negc"):
                    d[nm] = small.tile([P, 16], F32, tag=nm, name="%s%d" % (nm, b))
                bt[b] = d
            return bt[b]

        def hid_tile(g):
            if g not in hid:
                hid[g] = work.tile([P, 2 * 512], BF16, tag="hid", name="hid%d" % g, align_bytes=64)
            return hid[g]

        for op in plan:
            kind = op[0]
            if kind == "prep":
                b = op[1]
                tr = ps.tile([P, 512], F32, tag="lg", name="tr%d" % b)
                for j in range(4):
                    nc.tensor.transpose(out=tr[:, j * P : (j + 1) * P], in_=pmat[:, b, j * P : (j + 1) * P], identity=ident[:])
                e = const.tile([P, P, 4], F32, name="ed%d" % b)
                ed[b] = e
                nc.scalar.copy(out=e[:], in_=tr[:].rearrange("p (j n) -> p n j", j=4))
                nc.gpsimd.tensor_tensor(out=e[:, 0:64, :], in0=e[:, 0:64, :], in1=e[:, 96:97, :].to_broadcast([P, 64, 4]), op=ALU.add)
            elif kind == "padd":
                t = op[1]
                b = t // 16
                c0 = (t % 16) * P
                pb = ps.tile([P, 512], F32, tag="pb", bufs=2, name="pb%d" % t)
                pbank[t] = pb
                for j in range(4):
                    nc.tensor.matmul(out=pb[:, j * P : (j + 1) * P], lhsT=pmat[:, b, j * P : (j + 1) * P], rhs=sel[:, c0 : c0 + P], start=True, stop=True)
            elif kind == "ptanh":
                t = op[1]
                g = group_of[t]
                s = t - GROUPS[g][0]
                h = hid_tile(g)
                nc.scalar.activation(
                    out=h[:, s * 512 : (s + 1) * 512].rearrange("p (r j) -> p r j", j=4),
                    in_=pbank[t][:].rearrange("p (j r) -> p r j", j=4),
                    func=ACT.Tanh,
                )
            elif kind == "add":
                g = op[1]
                f, n = GROUPS[g]
                b = f // 16
                t0 = (f % 16) * 4
                nt = 4 * n
                pr = work.tile([P, 2 * 512], F32, tag="pre", bufs=2, name="pre%d" % g)
                pre[g] = pr
                eng = nc.vector if MODES[g] == "V" else nc.gpsimd
                eng.tensor_tensor(
                    out=pr[:, : nt * P].rearrange("p (t u j) -> p t u j", u=32, j=4),
                    in0=ed[b][:, 64:96, :].unsqueeze(1).to_broadcast([P, nt, 32, 4]),
                    in1=ed[b][:, t0 : t0 + nt, :].unsqueeze(2).to_broadcast([P, nt, 32, 4]),
                    op=ALU.add,
                )
            elif kind == "tanh":
                g = op[1]
                n = GROUPS[g][1]
                nc.scalar.activation(out=hid_tile(g)[:, : n * 512], in_=pre[g][:, : n * 512], func=ACT.Tanh)
            elif kind == "quant":
                g = op[1]
                n = GROUPS[g][1]
                hcod[g] = work.tile([P, 2 * P], U32, tag="hc", name="hc%d" % g, align_bytes=64)
                hsc[g] = work.tile([P, 2 * P], U8, tag="hs", name="hs%d" % g, align_bytes=64)
                nc.vector.quantize_mx(out=hcod[g][:, : n * P].bitcast(FP8X4), scales=hsc[g][:, : n * P], in_=hid[g][:, : n * 512])
            elif kind == "mx":
                t = op[1]
                g = group_of[t]
                s = t - GROUPS[g][0]
                for h in range(2):
                    acc = ps.tile([P, 512], F32, tag="lg", name="lg%d_%d" % (t, h))
                    lg[(t, h)] = acc
                    nc.tensor.matmul_mx(
                        out=acc[:],
                        lhsT=hcod[g][:, s * P : (s + 1) * P].bitcast(FP8X4),
                        lhsT_scale=hsc[g][:, s * P : (s + 1) * P],
                        rhs=w2c[:, h * 512 : (h + 1) * 512].bitcast(FP8X4),
                        rhs_scale=w2s[:, h * 512 : (h + 1) * 512],
                        start=True,
                        stop=True,
                    )
            elif kind == "ev":
                t, h = op[1], op[2]
                if h == 0:
                    zt[t] = zpool.tile([P, 1024], F32, tag="z", name="z%d" % t)
                nc.vector.tensor_tensor(out=zt[t][:, h * 512 : (h + 1) * 512], in0=lg[(t, h)][:], in1=b2_bc[:, h * 512 : (h + 1) * 512], op=ALU.add)
            elif kind == "red":
                t = op[1]
                b = batch_of[t]
                c = t - BATCHES[b][0]
                nc.vector.tensor_reduce(out=batch_tiles(b)["negm"][:, c : c + 1], in_=zt[t][:], axis=AX.X, op=ALU.max, negate=True)
            elif kind == "exp":
                t = op[1]
                b = batch_of[t]
                c = t - BATCHES[b][0]
                d = batch_tiles(b)
                junk = work.tile([P, 1024], BF16, tag="junk", bufs=2, name="junk%d" % t)
                nc.scalar.activation(out=junk[:], in_=zt[t][:], func=ACT.Exp, bias=d["negm"][:, c : c + 1], scale=1.0, accum_out=d["ssum"][:, c : c + 1])
            elif kind == "ln":
                b = op[1]
                n = BATCHES[b][1]
                d = batch_tiles(b)
                nc.scalar.activation(out=d["lns"][:, :n], in_=d["ssum"][:, :n], func=ACT.Ln)
            elif kind == "negc":
                b, t, n = op[1], op[2], op[3]
                c = t - BATCHES[b][0]
                d = batch_tiles(b)
                nc.vector.tensor_tensor(out=d["negc"][:, c : c + n], in0=d["negm"][:, c : c + n], in1=d["lns"][:, c : c + n], op=ALU.subtract)
            else:
                t = op[1]
                b = batch_of[t]
                c = t - BATCHES[b][0]
                negc = batch_tiles(b)["negc"][:, c : c + 1]
                who = LAST_FINS.get(t, "G")
                if who == "V":
                    nc.vector.tensor_scalar(out=zt[t][:], in0=zt[t][:], scalar1=negc, scalar2=None, op0=ALU.add)
                elif who == "S":
                    nc.scalar.activation(out=zt[t][:], in_=zt[t][:], func=ACT.Identity, bias=negc, scale=1.0)
                else:
                    nc.gpsimd.tensor_scalar(out=zt[t][:], in0=zt[t][:], scalar1=1.0, scalar2=negc, op0=ALU.mult, op1=ALU.add)
                nc.sync.dma_start(out=outf[t * P : (t + 1) * P, :], in_=zt[t][:])
